import numpy as np
import ml_dtypes

BF16 = ml_dtypes.bfloat16


def bf(x):
    return np.asarray(x, np.float32).astype(BF16)


def f32(x):
    return np.asarray(x, np.float32)


def f64(x):
    return np.asarray(x).astype(np.float64)


def striped(idx):
    return np.tile(idx.reshape(-1, 16).T, (8, 1))


D, S, L, F, M, H, E, N = 128, 1024, 2, 128, 256, 512, 1024, 2048


def setup_inputs():
    idx = np.concatenate([np.random.permutation(S)[:H] for _ in range(N // H)])
    return {"table": bf(np.random.standard_normal((D, S))), "w_src": bf(np.random.standard_normal((D, M)) / np.sqrt(D + D)), "w_dst": bf(np.random.standard_normal((D, M)) / np.sqrt(D + D)), "b1": f32(0.1 * np.random.standard_normal((M, 1))), "w2": bf(np.random.standard_normal((F, M)) / np.sqrt(F)), "b2": f32(0.1 * np.random.standard_normal((M, 1))), "offs": striped(idx)}


def reference(table, w_src, w_dst, b1, w2, b2, offs):
    idx = offs[:16].T.reshape(-1)
    t = f64(table)
    pre = f64(w_src).T @ t[:, idx[:E]] + f64(w_dst).T @ t[:, idx[E:]] + f64(b1)
    h = np.tanh(pre)
    w = f64(w2)
    proj = np.concatenate([w[:, l * F:(l + 1) * F].T @ h[l * F:(l + 1) * F] for l in range(L)], axis=0)
    return proj + f64(b2)

@@ -1,0 +1,57 @@
+import concourse.mybir as mybir
+
+BF16, F32, U16 = mybir.dt.bfloat16, mybir.dt.float32, mybir.dt.uint16
+TANH = mybir.ActivationFunctionType.Tanh
+
+P = 128
+NODES = 1024
+EDGES = 1024
+LAYERS = 2
+PIECE = 512
+PIECE_COLS = PIECE // 16
+TARGET_COL = EDGES // 16
+
+FLOPS = 2 * EDGES * (2 * P * LAYERS * P + LAYERS * P * P)
+
+
+def tile_quantumentanglementlayer_kernel(tc, table, w_src, w_dst, b1, w2, b2, offs, out):
+    nc = tc.nc
+    with (
+        tc.tile_pool(name="held", bufs=1) as held,
+        tc.tile_pool(name="hidden", bufs=4) as hidden,
+        tc.tile_pool(name="staged", bufs=4) as staged,
+        tc.psum_pool(name="pre_banks", bufs=4) as pre_banks,
+        tc.psum_pool(name="proj_banks", bufs=4) as proj_banks,
+    ):
+        offsets = held.tile([P, 2 * EDGES // 16], U16, name="offsets")
+        nc.sync.dma_start(offsets[:], offs)
+        nodes = held.tile([P, NODES], BF16, name="nodes")
+        nc.sync.dma_start(nodes[:], table)
+        src_map = held.tile([P, LAYERS * P], BF16, name="src_map")
+        nc.scalar.dma_start(src_map[:], w_src)
+        dst_map = held.tile([P, LAYERS * P], BF16, name="dst_map")
+        nc.scalar.dma_start(dst_map[:], w_dst)
+        second_map = held.tile([P, LAYERS * P], BF16, name="second_map")
+        nc.scalar.dma_start(second_map[:], w2)
+        bias1 = held.tile([P, LAYERS], F32, name="bias1")
+        bias2 = held.tile([P, LAYERS], F32, name="bias2")
+        with nc.allow_non_contiguous_dma(reason="a bias goes one value to a partition"):
+            nc.gpsimd.dma_start(bias1[:], b1.rearrange("(l p) o -> p (l o)", p=P))
+            nc.gpsimd.dma_start(bias2[:], b2.rearrange("(l p) o -> p (l o)", p=P))
+
+        for piece in range(EDGES // PIECE):
+            first = piece * PIECE_COLS
+            sources = offsets[:, first : first + PIECE_COLS]
+            targets = offsets[:, TARGET_COL + first : TARGET_COL + first + PIECE_COLS]
+            for layer in range(LAYERS):
+                rows = slice(layer * P, (layer + 1) * P)
+                pre = pre_banks.tile([P, PIECE], F32, name="pre")
+                nc.tensor.matmul(pre[:], src_map[:, rows], nodes[:].indirect(sources), start=True, stop=False)
+                nc.tensor.matmul(pre[:], dst_map[:, rows], nodes[:].indirect(targets), start=False, stop=True)
+                h = hidden.tile([P, PIECE], BF16, name="h")
+                nc.scalar.activation(h[:], pre[:], TANH, bias=bias1[:, layer : layer + 1])
+                proj = proj_banks.tile([P, PIECE], F32, name="proj")
+                nc.tensor.matmul(proj[:], second_map[:, rows], h[:], start=True, stop=True)
+                result = staged.tile([P, PIECE], F32, name="result")
+                nc.vector.tensor_scalar_add(result[:], proj[:], bias2[:, layer : layer + 1])
+                nc.sync.dma_start(out[rows, piece * PIECE : (piece + 1) * PIECE], result[:])

@@ -36,8 +36,8 @@ def tile_quantumentanglementlayer_kernel(tc, table, w_src, w_dst, b1, w2, b2, of
         bias1 = held.tile([P, LAYERS], F32, name="bias1")
         bias2 = held.tile([P, LAYERS], F32, name="bias2")
         with nc.allow_non_contiguous_dma(reason="a bias goes one value to a partition"):
-            nc.gpsimd.dma_start(bias1[:], b1.rearrange("(l p) o -> p (l o)", p=P))
-            nc.gpsimd.dma_start(bias2[:], b2.rearrange("(l p) o -> p (l o)", p=P))
+            nc.sync.dma_start(bias1[:], b1.rearrange("(l p) o -> p (l o)", p=P))
+            nc.sync.dma_start(bias2[:], b2.rearrange("(l p) o -> p (l o)", p=P))
 
         for piece in range(EDGES // PIECE):
             first = piece * PIECE_COLS

@@ -10,18 +10,19 @@ LAYERS = 2
 PIECE = 512
 PIECE_COLS = PIECE // 16
 TARGET_COL = EDGES // 16
+WARM_UP_MATMULS = 6
 
 FLOPS = 2 * EDGES * (2 * P * LAYERS * P + LAYERS * P * P)
 
 
 def tile_quantumentanglementlayer_kernel(tc, table, w_src, w_dst, b1, w2, b2, offs, out):
     nc = tc.nc
+    blocks = [(piece, layer) for piece in range(EDGES // PIECE) for layer in range(LAYERS)]
     with (
         tc.tile_pool(name="held", bufs=1) as held,
-        tc.tile_pool(name="hidden", bufs=4) as hidden,
-        tc.tile_pool(name="staged", bufs=4) as staged,
-        tc.psum_pool(name="pre_banks", bufs=4) as pre_banks,
-        tc.psum_pool(name="proj_banks", bufs=4) as proj_banks,
+        tc.tile_pool(name="staged", bufs=len(blocks)) as staged,
+        tc.psum_pool(name="pre_banks", bufs=len(blocks)) as pre_banks,
+        tc.psum_pool(name="proj_banks", bufs=len(blocks)) as proj_banks,
     ):
         offsets = held.tile([P, 2 * EDGES // 16], U16, name="offsets")
         nc.sync.dma_start(offsets[:], offs)
@@ -39,19 +40,29 @@ def tile_quantumentanglementlayer_kernel(tc, table, w_src, w_dst, b1, w2, b2, of
             nc.sync.dma_start(bias1[:], b1.rearrange("(l p) o -> p (l o)", p=P))
             nc.sync.dma_start(bias2[:], b2.rearrange("(l p) o -> p (l o)", p=P))
 
-        for piece in range(EDGES // PIECE):
+        zeros = held.tile([P, PIECE], BF16, name="zeros")
+        nc.vector.memset(zeros[:], 0.0)
+        unread = pre_banks.tile([P, PIECE], F32, name="pre")
+        for turn in range(WARM_UP_MATMULS):
+            nc.tensor.matmul(unread[:], zeros[:, :P], zeros[:], start=True, stop=True)
+
+        hidden = {}
+        for piece, layer in blocks:
             first = piece * PIECE_COLS
             sources = offsets[:, first : first + PIECE_COLS]
             targets = offsets[:, TARGET_COL + first : TARGET_COL + first + PIECE_COLS]
-            for layer in range(LAYERS):
-                rows = slice(layer * P, (layer + 1) * P)
-                pre = pre_banks.tile([P, PIECE], F32, name="pre")
-                nc.tensor.matmul(pre[:], src_map[:, rows], nodes[:].indirect(sources), start=True, stop=False)
-                nc.tensor.matmul(pre[:], dst_map[:, rows], nodes[:].indirect(targets), start=False, stop=True)
-                h = hidden.tile([P, PIECE], BF16, name="h")
-                nc.scalar.activation(h[:], pre[:], TANH, bias=bias1[:, layer : layer + 1])
-                proj = proj_banks.tile([P, PIECE], F32, name="proj")
-                nc.tensor.matmul(proj[:], second_map[:, rows], h[:], start=True, stop=True)
-                result = staged.tile([P, PIECE], F32, name="result")
-                nc.vector.tensor_scalar_add(result[:], proj[:], bias2[:, layer : layer + 1])
-                nc.sync.dma_start(out[rows, piece * PIECE : (piece + 1) * PIECE], result[:])
+            rows = slice(layer * P, (layer + 1) * P)
+            pre = pre_banks.tile([P, PIECE], F32, name="pre")
+            nc.tensor.matmul(pre[:], src_map[:, rows], nodes[:].indirect(sources), start=True, stop=False)
+            nc.tensor.matmul(pre[:], dst_map[:, rows], nodes[:].indirect(targets), start=False, stop=True)
+            h = held.tile([P, PIECE], BF16, name=f"h{piece}{layer}")
+            nc.scalar.activation(h[:], pre[:], TANH, bias=bias1[:, layer : layer + 1])
+            hidden[piece, layer] = h
+
+        for piece, layer in blocks:
+            rows = slice(layer * P, (layer + 1) * P)
+            proj = proj_banks.tile([P, PIECE], F32, name="proj")
+            nc.tensor.matmul(proj[:], second_map[:, rows], hidden[piece, layer][:], start=True, stop=True)
+            result = staged.tile([P, PIECE], F32, name="result")
+            nc.vector.tensor_scalar_add(result[:], proj[:], bias2[:, layer : layer + 1])
+            nc.sync.dma_start(out[rows, piece * PIECE : (piece + 1) * PIECE], result[:])

@@ -10,7 +10,7 @@ LAYERS = 2
 PIECE = 512
 PIECE_COLS = PIECE // 16
 TARGET_COL = EDGES // 16
-WARM_UP_MATMULS = 6
+WARM_UP_MATMULS = 3
 
 FLOPS = 2 * EDGES * (2 * P * LAYERS * P + LAYERS * P * P)
 

@@ -10,7 +10,6 @@ LAYERS = 2
 PIECE = 512
 PIECE_COLS = PIECE // 16
 TARGET_COL = EDGES // 16
-WARM_UP_MATMULS = 3
 
 FLOPS = 2 * EDGES * (2 * P * LAYERS * P + LAYERS * P * P)
 
@@ -25,26 +24,21 @@ def tile_quantumentanglementlayer_kernel(tc, table, w_src, w_dst, b1, w2, b2, of
         tc.psum_pool(name="proj_banks", bufs=len(blocks)) as proj_banks,
     ):
         offsets = held.tile([P, 2 * EDGES // 16], U16, name="offsets")
-        nc.sync.dma_start(offsets[:], offs)
         nodes = held.tile([P, NODES], BF16, name="nodes")
-        nc.sync.dma_start(nodes[:], table)
         src_map = held.tile([P, LAYERS * P], BF16, name="src_map")
-        nc.scalar.dma_start(src_map[:], w_src)
         dst_map = held.tile([P, LAYERS * P], BF16, name="dst_map")
-        nc.scalar.dma_start(dst_map[:], w_dst)
         second_map = held.tile([P, LAYERS * P], BF16, name="second_map")
+        nc.sync.dma_start(offsets[:], offs)
+        nc.scalar.dma_start(nodes[:, NODES // 2 :], table[:, NODES // 2 :])
+        nc.sync.dma_start(nodes[:, : NODES // 2], table[:, : NODES // 2])
+        nc.scalar.dma_start(src_map[:], w_src)
+        nc.sync.dma_start(dst_map[:], w_dst)
         nc.scalar.dma_start(second_map[:], w2)
         bias1 = held.tile([P, LAYERS], F32, name="bias1")
         bias2 = held.tile([P, LAYERS], F32, name="bias2")
         with nc.allow_non_contiguous_dma(reason="a bias goes one value to a partition"):
             nc.sync.dma_start(bias1[:], b1.rearrange("(l p) o -> p (l o)", p=P))
             nc.sync.dma_start(bias2[:], b2.rearrange("(l p) o -> p (l o)", p=P))
-
-        zeros = held.tile([P, PIECE], BF16, name="zeros")
-        nc.vector.memset(zeros[:], 0.0)
-        unread = pre_banks.tile([P, PIECE], F32, name="pre")
-        for turn in range(WARM_UP_MATMULS):
-            nc.tensor.matmul(unread[:], zeros[:, :P], zeros[:], start=True, stop=True)
 
         hidden = {}
         for piece, layer in blocks:

@@ -2,12 +2,14 @@ import concourse.mybir as mybir
 
 BF16, F32, U16 = mybir.dt.bfloat16, mybir.dt.float32, mybir.dt.uint16
 TANH = mybir.ActivationFunctionType.Tanh
+IDENTITY = mybir.ActivationFunctionType.Identity
 
 P = 128
 NODES = 1024
 EDGES = 1024
 LAYERS = 2
 PIECE = 512
+HALF = PIECE // 2
 PIECE_COLS = PIECE // 16
 TARGET_COL = EDGES // 16
 
@@ -19,20 +21,19 @@ def tile_quantumentanglementlayer_kernel(tc, table, w_src, w_dst, b1, w2, b2, of
     blocks = [(piece, layer) for piece in range(EDGES // PIECE) for layer in range(LAYERS)]
     with (
         tc.tile_pool(name="held", bufs=1) as held,
-        tc.tile_pool(name="staged", bufs=len(blocks)) as staged,
+        tc.tile_pool(name="staged", bufs=2 * len(blocks)) as staged,
         tc.psum_pool(name="pre_banks", bufs=len(blocks)) as pre_banks,
         tc.psum_pool(name="proj_banks", bufs=len(blocks)) as proj_banks,
     ):
         offsets = held.tile([P, 2 * EDGES // 16], U16, name="offsets")
-        nodes = held.tile([P, NODES], BF16, name="nodes")
-        src_map = held.tile([P, LAYERS * P], BF16, name="src_map")
-        dst_map = held.tile([P, LAYERS * P], BF16, name="dst_map")
-        second_map = held.tile([P, LAYERS * P], BF16, name="second_map")
         nc.sync.dma_start(offsets[:], offs)
-        nc.scalar.dma_start(nodes[:, NODES // 2 :], table[:, NODES // 2 :])
-        nc.sync.dma_start(nodes[:, : NODES // 2], table[:, : NODES // 2])
+        nodes = held.tile([P, NODES], BF16, name="nodes")
+        nc.sync.dma_start(nodes[:], table)
+        src_map = held.tile([P, LAYERS * P], BF16, name="src_map")
         nc.scalar.dma_start(src_map[:], w_src)
-        nc.sync.dma_start(dst_map[:], w_dst)
+        dst_map = held.tile([P, LAYERS * P], BF16, name="dst_map")
+        nc.scalar.dma_start(dst_map[:], w_dst)
+        second_map = held.tile([P, LAYERS * P], BF16, name="second_map")
         nc.scalar.dma_start(second_map[:], w2)
         bias1 = held.tile([P, LAYERS], F32, name="bias1")
         bias2 = held.tile([P, LAYERS], F32, name="bias2")
@@ -55,8 +56,16 @@ def tile_quantumentanglementlayer_kernel(tc, table, w_src, w_dst, b1, w2, b2, of
 
         for piece, layer in blocks:
             rows = slice(layer * P, (layer + 1) * P)
-            proj = proj_banks.tile([P, PIECE], F32, name="proj")
-            nc.tensor.matmul(proj[:], second_map[:, rows], hidden[piece, layer][:], start=True, stop=True)
-            result = staged.tile([P, PIECE], F32, name="result")
-            nc.vector.tensor_scalar_add(result[:], proj[:], bias2[:, layer : layer + 1])
-            nc.sync.dma_start(out[rows, piece * PIECE : (piece + 1) * PIECE], result[:])
+            shift = bias2[:, layer : layer + 1]
+            for half in range(2):
+                proj = proj_banks.tile([P, HALF], F32, name="proj")
+                h_half = hidden[piece, layer][:, half * HALF : (half + 1) * HALF]
+                nc.tensor.matmul(proj[:], second_map[:, rows], h_half, start=True, stop=True)
+                result = staged.tile([P, HALF], F32, name="result")
+                first_edge = piece * PIECE + half * HALF
+                if half == 0:
+                    nc.vector.tensor_scalar_add(result[:], proj[:], shift)
+                    nc.sync.dma_start(out[rows, first_edge : first_edge + HALF], result[:])
+                else:
+                    nc.scalar.activation(result[:], proj[:], IDENTITY, bias=shift)
+                    nc.scalar.dma_start(out[rows, first_edge : first_edge + HALF], result[:])

@@ -8,22 +8,23 @@ P = 128
 NODES = 1024
 EDGES = 1024
 LAYERS = 2
-PIECE = 512
-HALF = PIECE // 2
+PIECE = 256
+PIECES = EDGES // PIECE
 PIECE_COLS = PIECE // 16
 TARGET_COL = EDGES // 16
+PSUM_BANKS = 8
+FIRST_RUN = PIECES - 1
+CHUNK = 64
 
 FLOPS = 2 * EDGES * (2 * P * LAYERS * P + LAYERS * P * P)
 
 
 def tile_quantumentanglementlayer_kernel(tc, table, w_src, w_dst, b1, w2, b2, offs, out):
     nc = tc.nc
-    blocks = [(piece, layer) for piece in range(EDGES // PIECE) for layer in range(LAYERS)]
     with (
         tc.tile_pool(name="held", bufs=1) as held,
-        tc.tile_pool(name="staged", bufs=2 * len(blocks)) as staged,
-        tc.psum_pool(name="pre_banks", bufs=len(blocks)) as pre_banks,
-        tc.psum_pool(name="proj_banks", bufs=len(blocks)) as proj_banks,
+        tc.tile_pool(name="staged", bufs=PIECES * LAYERS) as staged,
+        tc.psum_pool(name="banks", bufs=PSUM_BANKS) as banks,
     ):
         offsets = held.tile([P, 2 * EDGES // 16], U16, name="offsets")
         nc.sync.dma_start(offsets[:], offs)
@@ -42,30 +43,44 @@ def tile_quantumentanglementlayer_kernel(tc, table, w_src, w_dst, b1, w2, b2, of
             nc.sync.dma_start(bias2[:], b2.rearrange("(l p) o -> p (l o)", p=P))
 
         hidden = {}
-        for piece, layer in blocks:
+
+        def look_up(piece):
             first = piece * PIECE_COLS
             sources = offsets[:, first : first + PIECE_COLS]
             targets = offsets[:, TARGET_COL + first : TARGET_COL + first + PIECE_COLS]
-            rows = slice(layer * P, (layer + 1) * P)
-            pre = pre_banks.tile([P, PIECE], F32, name="pre")
-            nc.tensor.matmul(pre[:], src_map[:, rows], nodes[:].indirect(sources), start=True, stop=False)
-            nc.tensor.matmul(pre[:], dst_map[:, rows], nodes[:].indirect(targets), start=False, stop=True)
-            h = held.tile([P, PIECE], BF16, name=f"h{piece}{layer}")
-            nc.scalar.activation(h[:], pre[:], TANH, bias=bias1[:, layer : layer + 1])
-            hidden[piece, layer] = h
+            for layer in range(LAYERS):
+                rows = slice(layer * P, (layer + 1) * P)
+                pre = banks.tile([P, PIECE], F32, name="pre", tag="bank")
+                nc.tensor.matmul(pre[:], src_map[:, rows], nodes[:].indirect(sources), start=True, stop=False)
+                nc.tensor.matmul(pre[:], dst_map[:, rows], nodes[:].indirect(targets), start=False, stop=True)
+                h = held.tile([P, PIECE], BF16, name=f"h{piece}{layer}")
+                nc.scalar.activation(h[:], pre[:], TANH, bias=bias1[:, layer : layer + 1])
+                hidden[piece, layer] = h
 
-        for piece, layer in blocks:
-            rows = slice(layer * P, (layer + 1) * P)
-            shift = bias2[:, layer : layer + 1]
-            for half in range(2):
-                proj = proj_banks.tile([P, HALF], F32, name="proj")
-                h_half = hidden[piece, layer][:, half * HALF : (half + 1) * HALF]
-                nc.tensor.matmul(proj[:], second_map[:, rows], h_half, start=True, stop=True)
-                result = staged.tile([P, HALF], F32, name="result")
-                first_edge = piece * PIECE + half * HALF
-                if half == 0:
+        def project(piece):
+            edges = slice(piece * PIECE, (piece + 1) * PIECE)
+            for layer in range(LAYERS):
+                rows = slice(layer * P, (layer + 1) * P)
+                shift = bias2[:, layer : layer + 1]
+                proj = banks.tile([P, PIECE], F32, name="proj", tag="bank")
+                for start in range(0, PIECE, CHUNK):
+                    chunk = slice(start, start + CHUNK)
+                    nc.tensor.matmul(
+                        proj[:, chunk], second_map[:, rows], hidden[piece, layer][:, chunk], start=True, stop=True
+                    )
+                result = staged.tile([P, PIECE], F32, name="result")
+                if layer == 0:
                     nc.vector.tensor_scalar_add(result[:], proj[:], shift)
-                    nc.sync.dma_start(out[rows, first_edge : first_edge + HALF], result[:])
+                    nc.sync.dma_start(out[rows, edges], result[:])
                 else:
                     nc.scalar.activation(result[:], proj[:], IDENTITY, bias=shift)
-                    nc.scalar.dma_start(out[rows, first_edge : first_edge + HALF], result[:])
+                    nc.scalar.dma_start(out[rows, edges], result[:])
+
+        for piece in range(FIRST_RUN):
+            look_up(piece)
+        for piece in range(FIRST_RUN):
+            project(piece)
+        for piece in range(FIRST_RUN, PIECES):
+            look_up(piece)
+        for piece in range(FIRST_RUN, PIECES):
+            project(piece)

@@ -71,10 +71,9 @@ def tile_quantumentanglementlayer_kernel(tc, table, w_src, w_dst, b1, w2, b2, of
                 result = staged.tile([P, PIECE], F32, name="result")
                 if layer == 0:
                     nc.vector.tensor_scalar_add(result[:], proj[:], shift)
-                    nc.sync.dma_start(out[rows, edges], result[:])
                 else:
                     nc.scalar.activation(result[:], proj[:], IDENTITY, bias=shift)
-                    nc.scalar.dma_start(out[rows, edges], result[:])
+                nc.sync.dma_start(out[rows, edges], result[:])
 
         for piece in range(FIRST_RUN):
             look_up(piece)

@@ -14,7 +14,8 @@ PIECE_COLS = PIECE // 16
 TARGET_COL = EDGES // 16
 PSUM_BANKS = 8
 FIRST_RUN = PIECES - 1
-CHUNK = 64
+BETWEEN = 2
+CHUNK = 44
 
 FLOPS = 2 * EDGES * (2 * P * LAYERS * P + LAYERS * P * P)
 
@@ -57,14 +58,14 @@ def tile_quantumentanglementlayer_kernel(tc, table, w_src, w_dst, b1, w2, b2, of
                 nc.scalar.activation(h[:], pre[:], TANH, bias=bias1[:, layer : layer + 1])
                 hidden[piece, layer] = h
 
-        def project(piece):
+        def project(piece, width):
             edges = slice(piece * PIECE, (piece + 1) * PIECE)
             for layer in range(LAYERS):
                 rows = slice(layer * P, (layer + 1) * P)
                 shift = bias2[:, layer : layer + 1]
                 proj = banks.tile([P, PIECE], F32, name="proj", tag="bank")
-                for start in range(0, PIECE, CHUNK):
-                    chunk = slice(start, start + CHUNK)
+                for start in range(0, PIECE, width):
+                    chunk = slice(start, min(start + width, PIECE))
                     nc.tensor.matmul(
                         proj[:, chunk], second_map[:, rows], hidden[piece, layer][:, chunk], start=True, stop=True
                     )
@@ -77,9 +78,9 @@ def tile_quantumentanglementlayer_kernel(tc, table, w_src, w_dst, b1, w2, b2, of
 
         for piece in range(FIRST_RUN):
             look_up(piece)
-        for piece in range(FIRST_RUN):
-            project(piece)
+        for piece in range(BETWEEN):
+            project(piece, CHUNK)
         for piece in range(FIRST_RUN, PIECES):
             look_up(piece)
-        for piece in range(FIRST_RUN, PIECES):
-            project(piece)
+        for piece in range(BETWEEN, PIECES):
+            project(piece, PIECE)

@@ -8,13 +8,10 @@ P = 128
 NODES = 1024
 EDGES = 1024
 LAYERS = 2
-PIECE = 256
-PIECES = EDGES // PIECE
-PIECE_COLS = PIECE // 16
 TARGET_COL = EDGES // 16
 PSUM_BANKS = 8
-FIRST_RUN = PIECES - 1
-BETWEEN = 2
+BLOCK = 512
+STRIP = 256
 CHUNK = 44
 
 FLOPS = 2 * EDGES * (2 * P * LAYERS * P + LAYERS * P * P)
@@ -24,7 +21,7 @@ def tile_quantumentanglementlayer_kernel(tc, table, w_src, w_dst, b1, w2, b2, of
     nc = tc.nc
     with (
         tc.tile_pool(name="held", bufs=1) as held,
-        tc.tile_pool(name="staged", bufs=PIECES * LAYERS) as staged,
+        tc.tile_pool(name="staged", bufs=LAYERS * EDGES // STRIP) as staged,
         tc.psum_pool(name="banks", bufs=PSUM_BANKS) as banks,
     ):
         offsets = held.tile([P, 2 * EDGES // 16], U16, name="offsets")
@@ -43,44 +40,42 @@ def tile_quantumentanglementlayer_kernel(tc, table, w_src, w_dst, b1, w2, b2, of
             nc.sync.dma_start(bias1[:], b1.rearrange("(l p) o -> p (l o)", p=P))
             nc.sync.dma_start(bias2[:], b2.rearrange("(l p) o -> p (l o)", p=P))
 
-        hidden = {}
+        hidden = [held.tile([P, EDGES], BF16, name=f"hidden{layer}") for layer in range(LAYERS)]
 
-        def look_up(piece):
-            first = piece * PIECE_COLS
-            sources = offsets[:, first : first + PIECE_COLS]
-            targets = offsets[:, TARGET_COL + first : TARGET_COL + first + PIECE_COLS]
-            for layer in range(LAYERS):
-                rows = slice(layer * P, (layer + 1) * P)
-                pre = banks.tile([P, PIECE], F32, name="pre", tag="bank")
-                nc.tensor.matmul(pre[:], src_map[:, rows], nodes[:].indirect(sources), start=True, stop=False)
-                nc.tensor.matmul(pre[:], dst_map[:, rows], nodes[:].indirect(targets), start=False, stop=True)
-                h = held.tile([P, PIECE], BF16, name=f"h{piece}{layer}")
-                nc.scalar.activation(h[:], pre[:], TANH, bias=bias1[:, layer : layer + 1])
-                hidden[piece, layer] = h
+        def look_up(layer, edge, width):
+            rows = slice(layer * P, (layer + 1) * P)
+            first, columns = edge // 16, width // 16
+            sources = offsets[:, first : first + columns]
+            targets = offsets[:, TARGET_COL + first : TARGET_COL + first + columns]
+            pre = banks.tile([P, width], F32, name="pre", tag="bank")
+            nc.tensor.matmul(pre[:], src_map[:, rows], nodes[:].indirect(sources), start=True, stop=False)
+            nc.tensor.matmul(pre[:], dst_map[:, rows], nodes[:].indirect(targets), start=False, stop=True)
+            nc.scalar.activation(
+                hidden[layer][:, edge : edge + width], pre[:], TANH, bias=bias1[:, layer : layer + 1]
+            )
 
-        def project(piece, width):
-            edges = slice(piece * PIECE, (piece + 1) * PIECE)
-            for layer in range(LAYERS):
-                rows = slice(layer * P, (layer + 1) * P)
-                shift = bias2[:, layer : layer + 1]
-                proj = banks.tile([P, PIECE], F32, name="proj", tag="bank")
-                for start in range(0, PIECE, width):
-                    chunk = slice(start, min(start + width, PIECE))
-                    nc.tensor.matmul(
-                        proj[:, chunk], second_map[:, rows], hidden[piece, layer][:, chunk], start=True, stop=True
-                    )
-                result = staged.tile([P, PIECE], F32, name="result")
-                if layer == 0:
-                    nc.vector.tensor_scalar_add(result[:], proj[:], shift)
-                else:
+        def project(layer, block, width):
+            rows = slice(layer * P, (layer + 1) * P)
+            shift = bias2[:, layer : layer + 1]
+            for edge in range(block, block + BLOCK, STRIP):
+                proj = banks.tile([P, STRIP], F32, name="proj", tag="bank")
+                for start in range(0, STRIP, width):
+                    stop = min(start + width, STRIP)
+                    moving = hidden[layer][:, edge + start : edge + stop]
+                    nc.tensor.matmul(proj[:, start:stop], second_map[:, rows], moving, start=True, stop=True)
+                result = staged.tile([P, STRIP], F32, name="result")
+                if layer == 1 and edge > block:
                     nc.scalar.activation(result[:], proj[:], IDENTITY, bias=shift)
-                nc.sync.dma_start(out[rows, edges], result[:])
+                else:
+                    nc.vector.tensor_scalar_add(result[:], proj[:], shift)
+                nc.sync.dma_start(out[rows, edge : edge + STRIP], result[:])
 
-        for piece in range(FIRST_RUN):
-            look_up(piece)
-        for piece in range(BETWEEN):
-            project(piece, CHUNK)
-        for piece in range(FIRST_RUN, PIECES):
-            look_up(piece)
-        for piece in range(BETWEEN, PIECES):
-            project(piece, PIECE)
+        look_up(0, 0, BLOCK)
+        look_up(1, 0, BLOCK)
+        look_up(0, BLOCK, BLOCK)
+        for layer in range(LAYERS):
+            project(layer, 0, CHUNK)
+        for edge in range(BLOCK, EDGES, STRIP):
+            look_up(1, edge, STRIP)
+        for layer in range(LAYERS):
+            project(layer, BLOCK, STRIP)

@@ -12,6 +12,7 @@ TARGET_COL = EDGES // 16
 PSUM_BANKS = 8
 BLOCK = 512
 STRIP = 256
+HALF = STRIP // 2
 CHUNK = 44
 
 FLOPS = 2 * EDGES * (2 * P * LAYERS * P + LAYERS * P * P)
@@ -21,7 +22,7 @@ def tile_quantumentanglementlayer_kernel(tc, table, w_src, w_dst, b1, w2, b2, of
     nc = tc.nc
     with (
         tc.tile_pool(name="held", bufs=1) as held,
-        tc.tile_pool(name="staged", bufs=LAYERS * EDGES // STRIP) as staged,
+        tc.tile_pool(name="staged", bufs=LAYERS * EDGES // STRIP + 1) as staged,
         tc.psum_pool(name="banks", bufs=PSUM_BANKS) as banks,
     ):
         offsets = held.tile([P, 2 * EDGES // 16], U16, name="offsets")
@@ -42,7 +43,7 @@ def tile_quantumentanglementlayer_kernel(tc, table, w_src, w_dst, b1, w2, b2, of
 
         hidden = [held.tile([P, EDGES], BF16, name=f"hidden{layer}") for layer in range(LAYERS)]
 
-        def look_up(layer, edge, width):
+        def look_up(layer, edge, width, step):
             rows = slice(layer * P, (layer + 1) * P)
             first, columns = edge // 16, width // 16
             sources = offsets[:, first : first + columns]
@@ -50,32 +51,35 @@ def tile_quantumentanglementlayer_kernel(tc, table, w_src, w_dst, b1, w2, b2, of
             pre = banks.tile([P, width], F32, name="pre", tag="bank")
             nc.tensor.matmul(pre[:], src_map[:, rows], nodes[:].indirect(sources), start=True, stop=False)
             nc.tensor.matmul(pre[:], dst_map[:, rows], nodes[:].indirect(targets), start=False, stop=True)
-            nc.scalar.activation(
-                hidden[layer][:, edge : edge + width], pre[:], TANH, bias=bias1[:, layer : layer + 1]
-            )
+            for start in range(0, width, step):
+                h = hidden[layer][:, edge + start : edge + start + step]
+                nc.scalar.activation(h, pre[:, start : start + step], TANH, bias=bias1[:, layer : layer + 1])
 
-        def project(layer, block, width):
+        def project(layer, edge, width, step, add_on_scalar):
             rows = slice(layer * P, (layer + 1) * P)
             shift = bias2[:, layer : layer + 1]
-            for edge in range(block, block + BLOCK, STRIP):
-                proj = banks.tile([P, STRIP], F32, name="proj", tag="bank")
-                for start in range(0, STRIP, width):
-                    stop = min(start + width, STRIP)
-                    moving = hidden[layer][:, edge + start : edge + stop]
-                    nc.tensor.matmul(proj[:, start:stop], second_map[:, rows], moving, start=True, stop=True)
-                result = staged.tile([P, STRIP], F32, name="result")
-                if layer == 1 and edge > block:
-                    nc.scalar.activation(result[:], proj[:], IDENTITY, bias=shift)
-                else:
-                    nc.vector.tensor_scalar_add(result[:], proj[:], shift)
-                nc.sync.dma_start(out[rows, edge : edge + STRIP], result[:])
+            proj = banks.tile([P, width], F32, name="proj", tag="bank")
+            for start in range(0, width, step):
+                stop = min(start + step, width)
+                moving = hidden[layer][:, edge + start : edge + stop]
+                nc.tensor.matmul(proj[:, start:stop], second_map[:, rows], moving, start=True, stop=True)
+            result = staged.tile([P, width], F32, name="result")
+            if add_on_scalar:
+                nc.scalar.activation(result[:], proj[:], IDENTITY, bias=shift)
+            else:
+                nc.vector.tensor_scalar_add(result[:], proj[:], shift)
+            nc.sync.dma_start(out[rows, edge : edge + width], result[:])
 
-        look_up(0, 0, BLOCK)
-        look_up(1, 0, BLOCK)
-        look_up(0, BLOCK, BLOCK)
+        look_up(0, 0, BLOCK, BLOCK)
+        look_up(1, 0, BLOCK, BLOCK)
+        look_up(0, BLOCK, BLOCK, STRIP)
         for layer in range(LAYERS):
-            project(layer, 0, CHUNK)
-        for edge in range(BLOCK, EDGES, STRIP):
-            look_up(1, edge, STRIP)
-        for layer in range(LAYERS):
-            project(layer, BLOCK, STRIP)
+            project(layer, 0, STRIP, CHUNK, add_on_scalar=False)
+            project(layer, STRIP, STRIP, CHUNK, add_on_scalar=layer == 1)
+        project(0, BLOCK, STRIP, STRIP, add_on_scalar=False)
+        look_up(1, BLOCK, STRIP, STRIP)
+        look_up(1, BLOCK + STRIP, STRIP, HALF)
+        project(0, BLOCK + STRIP, STRIP, STRIP, add_on_scalar=False)
+        project(1, BLOCK, STRIP, STRIP, add_on_scalar=False)
+        project(1, EDGES - STRIP, HALF, HALF, add_on_scalar=False)
+        project(1, EDGES - HALF, HALF, HALF, add_on_scalar=True)

@@ -41,6 +41,11 @@ def tile_quantumentanglementlayer_kernel(tc, table, w_src, w_dst, b1, w2, b2, of
             nc.sync.dma_start(bias1[:], b1.rearrange("(l p) o -> p (l o)", p=P))
             nc.sync.dma_start(bias2[:], b2.rearrange("(l p) o -> p (l o)", p=P))
 
+        zero = held.tile([P, 8], F32, name="zero")
+        nc.vector.memset(zero[:], 0.0)
+        zero_tanh = held.tile([P, 8], F32, name="zero_tanh")
+        nc.scalar.activation(zero_tanh[:], zero[:], TANH)
+
         hidden = [held.tile([P, EDGES], BF16, name=f"hidden{layer}") for layer in range(LAYERS)]
 
         def look_up(layer, edge, width, step):

@@ -13,7 +13,7 @@ PSUM_BANKS = 8
 BLOCK = 512
 STRIP = 256
 HALF = STRIP // 2
-CHUNK = 44
+CHUNK = 48
 
 FLOPS = 2 * EDGES * (2 * P * LAYERS * P + LAYERS * P * P)
 
@@ -79,12 +79,12 @@ def tile_quantumentanglementlayer_kernel(tc, table, w_src, w_dst, b1, w2, b2, of
         look_up(1, 0, BLOCK, BLOCK)
         look_up(0, BLOCK, BLOCK, STRIP)
         for layer in range(LAYERS):
-            project(layer, 0, STRIP, CHUNK, add_on_scalar=False)
-            project(layer, STRIP, STRIP, CHUNK, add_on_scalar=layer == 1)
+            for edge in range(0, BLOCK, STRIP):
+                project(layer, edge, STRIP, CHUNK, add_on_scalar=layer == 1)
         project(0, BLOCK, STRIP, STRIP, add_on_scalar=False)
         look_up(1, BLOCK, STRIP, STRIP)
         look_up(1, BLOCK + STRIP, STRIP, HALF)
         project(0, BLOCK + STRIP, STRIP, STRIP, add_on_scalar=False)
-        project(1, BLOCK, STRIP, STRIP, add_on_scalar=False)
+        project(1, BLOCK, STRIP, STRIP, add_on_scalar=True)
         project(1, EDGES - STRIP, HALF, HALF, add_on_scalar=False)
         project(1, EDGES - HALF, HALF, HALF, add_on_scalar=True)

@@ -33,13 +33,13 @@ def tile_quantumentanglementlayer_kernel(tc, table, w_src, w_dst, b1, w2, b2, of
         nc.scalar.dma_start(src_map[:], w_src)
         dst_map = held.tile([P, LAYERS * P], BF16, name="dst_map")
         nc.scalar.dma_start(dst_map[:], w_dst)
-        second_map = held.tile([P, LAYERS * P], BF16, name="second_map")
-        nc.scalar.dma_start(second_map[:], w2)
         bias1 = held.tile([P, LAYERS], F32, name="bias1")
         bias2 = held.tile([P, LAYERS], F32, name="bias2")
         with nc.allow_non_contiguous_dma(reason="a bias goes one value to a partition"):
             nc.sync.dma_start(bias1[:], b1.rearrange("(l p) o -> p (l o)", p=P))
             nc.sync.dma_start(bias2[:], b2.rearrange("(l p) o -> p (l o)", p=P))
+        second_map = held.tile([P, LAYERS * P], BF16, name="second_map")
+        nc.sync.dma_start(second_map[:], w2)
 
         zero = held.tile([P, 8], F32, name="zero")
         nc.vector.memset(zero[:], 0.0)
@@ -77,7 +77,8 @@ def tile_quantumentanglementlayer_kernel(tc, table, w_src, w_dst, b1, w2, b2, of
 
         look_up(0, 0, BLOCK, BLOCK)
         look_up(1, 0, BLOCK, BLOCK)
-        look_up(0, BLOCK, BLOCK, STRIP)
+        for edge in range(BLOCK, EDGES, STRIP):
+            look_up(0, edge, STRIP, STRIP)
         for layer in range(LAYERS):
             for edge in range(0, BLOCK, STRIP):
                 project(layer, edge, STRIP, CHUNK, add_on_scalar=layer == 1)

@@ -77,8 +77,7 @@ def tile_quantumentanglementlayer_kernel(tc, table, w_src, w_dst, b1, w2, b2, of
 
         look_up(0, 0, BLOCK, BLOCK)
         look_up(1, 0, BLOCK, BLOCK)
-        for edge in range(BLOCK, EDGES, STRIP):
-            look_up(0, edge, STRIP, STRIP)
+        look_up(0, BLOCK, BLOCK, STRIP)
         for layer in range(LAYERS):
             for edge in range(0, BLOCK, STRIP):
                 project(layer, edge, STRIP, CHUNK, add_on_scalar=layer == 1)

import concourse.mybir as mybir

BF16, F32, U16 = mybir.dt.bfloat16, mybir.dt.float32, mybir.dt.uint16
TANH = mybir.ActivationFunctionType.Tanh
IDENTITY = mybir.ActivationFunctionType.Identity

P = 128
NODES = 1024
EDGES = 1024
LAYERS = 2
TARGET_COL = EDGES // 16
PSUM_BANKS = 8
BLOCK = 512
STRIP = 256
HALF = STRIP // 2
CHUNK = 48

FLOPS = 2 * EDGES * (2 * P * LAYERS * P + LAYERS * P * P)


def tile_quantumentanglementlayer_kernel(tc, table, w_src, w_dst, b1, w2, b2, offs, out):
    nc = tc.nc
    with (
        tc.tile_pool(name="held", bufs=1) as held,
        tc.tile_pool(name="staged", bufs=LAYERS * EDGES // STRIP + 1) as staged,
        tc.psum_pool(name="banks", bufs=PSUM_BANKS) as banks,
    ):
        offsets = held.tile([P, 2 * EDGES // 16], U16, name="offsets")
        nc.sync.dma_start(offsets[:], offs)
        nodes = held.tile([P, NODES], BF16, name="nodes")
        nc.sync.dma_start(nodes[:], table)
        src_map = held.tile([P, LAYERS * P], BF16, name="src_map")
        nc.scalar.dma_start(src_map[:], w_src)
        dst_map = held.tile([P, LAYERS * P], BF16, name="dst_map")
        nc.scalar.dma_start(dst_map[:], w_dst)
        bias1 = held.tile([P, LAYERS], F32, name="bias1")
        bias2 = held.tile([P, LAYERS], F32, name="bias2")
        with nc.allow_non_contiguous_dma(reason="a bias goes one value to a partition"):
            nc.sync.dma_start(bias1[:], b1.rearrange("(l p) o -> p (l o)", p=P))
            nc.sync.dma_start(bias2[:], b2.rearrange("(l p) o -> p (l o)", p=P))
        second_map = held.tile([P, LAYERS * P], BF16, name="second_map")
        nc.sync.dma_start(second_map[:], w2)

        zero = held.tile([P, 8], F32, name="zero")
        nc.vector.memset(zero[:], 0.0)
        zero_tanh = held.tile([P, 8], F32, name="zero_tanh")
        nc.scalar.activation(zero_tanh[:], zero[:], TANH)

        hidden = [held.tile([P, EDGES], BF16, name=f"hidden{layer}") for layer in range(LAYERS)]

        def look_up(layer, edge, width, step):
            rows = slice(layer * P, (layer + 1) * P)
            first, columns = edge // 16, width // 16
            sources = offsets[:, first : first + columns]
            targets = offsets[:, TARGET_COL + first : TARGET_COL + first + columns]
            pre = banks.tile([P, width], F32, name="pre", tag="bank")
            nc.tensor.matmul(pre[:], src_map[:, rows], nodes[:].indirect(sources), start=True, stop=False)
            nc.tensor.matmul(pre[:], dst_map[:, rows], nodes[:].indirect(targets), start=False, stop=True)
            for start in range(0, width, step):
                h = hidden[layer][:, edge + start : edge + start + step]
                nc.scalar.activation(h, pre[:, start : start + step], TANH, bias=bias1[:, layer : layer + 1])

        def project(layer, edge, width, step, add_on_scalar):
            rows = slice(layer * P, (layer + 1) * P)
            shift = bias2[:, layer : layer + 1]
            proj = banks.tile([P, width], F32, name="proj", tag="bank")
            for start in range(0, width, step):
                stop = min(start + step, width)
                moving = hidden[layer][:, edge + start : edge + stop]
                nc.tensor.matmul(proj[:, start:stop], second_map[:, rows], moving, start=True, stop=True)
            result = staged.tile([P, width], F32, name="result")
            if add_on_scalar:
                nc.scalar.activation(result[:], proj[:], IDENTITY, bias=shift)
            else:
                nc.vector.tensor_scalar_add(result[:], proj[:], shift)
            nc.sync.dma_start(out[rows, edge : edge + width], result[:])

        look_up(0, 0, BLOCK, BLOCK)
        look_up(1, 0, BLOCK, BLOCK)
        look_up(0, BLOCK, BLOCK, STRIP)
        for layer in range(LAYERS):
            for edge in range(0, BLOCK, STRIP):
                project(layer, edge, STRIP, CHUNK, add_on_scalar=layer == 1)
        project(0, BLOCK, STRIP, STRIP, add_on_scalar=False)
        look_up(1, BLOCK, STRIP, STRIP)
        look_up(1, BLOCK + STRIP, STRIP, HALF)
        project(0, BLOCK + STRIP, STRIP, STRIP, add_on_scalar=False)
        project(1, BLOCK, STRIP, STRIP, add_on_scalar=True)
        project(1, EDGES - STRIP, HALF, HALF, add_on_scalar=False)
        project(1, EDGES - HALF, HALF, HALF, add_on_scalar=True)
